import numpy as np
import ml_dtypes


def mxq(x, axis, fmt="e4m3"):
    dtype, down = {"e4m3": (ml_dtypes.float8_e4m3fn, 7), "e5m2": (ml_dtypes.float8_e5m2, 14)}[fmt]
    v = np.moveaxis(np.asarray(x, np.float32).astype(ml_dtypes.bfloat16).astype(np.float64), axis, -1)
    blocks = v.reshape(v.shape[:-1] + (-1, 32))
    amax = np.abs(blocks).max(-1, keepdims=True)
    byte = np.maximum(np.where(amax > 0, np.frexp(amax)[1] - 1 + 127, 0) - down, 1)
    scale = np.exp2(byte - 127.0)
    codes = (blocks / scale).astype(np.float32).astype(dtype).astype(np.float64)
    return np.moveaxis((codes * scale).reshape(v.shape), -1, axis)


WIDE = False


def mx_kscale(k):
    if not WIDE:
        return np.ones(k)
    levels = np.array([10, -10, 5, -5, 0])
    if k % 512:
        return np.exp2(np.random.permutation(np.resize(levels, k // 32))).repeat(32)
    a = np.empty((k // 512, 16))
    for p in range(k // 512):
        a[p, :8] = np.random.permutation(np.resize(levels, 8))
        for g in range(8):
            far = levels[np.abs(levels - a[p, g]) >= 10]
            a[p, g + 8] = far[np.random.randint(len(far))]
    return np.exp2(a.ravel()).repeat(32)


BF16 = ml_dtypes.bfloat16


def bf(x):
    return np.asarray(x, np.float32).astype(BF16)


def f64(x):
    return np.asarray(x).astype(np.float64)


B, N, C, H = 2, 128, 2048, 16
EPS = 1e-6


def rmsnorm(v, w):
    var = np.mean(np.square(v), axis=-1, keepdims=True)
    return v * (1.0 / np.sqrt(var + EPS)) * w


def setup_inputs():
    s = mx_kscale(C)
    return {"x": bf(np.random.standard_normal((B, N, C)) * s),
            "w_qkv": bf(np.random.standard_normal((3 * C, C)) / np.sqrt(C) / s[None, :]),
            "q_norm_w": bf(1.0 + 0.1 * np.random.standard_normal(C)),
            "k_norm_w": bf(1.0 + 0.1 * np.random.standard_normal(C))}


def reference(x, w_qkv, q_norm_w, k_norm_w):
    xq = mxq(f64(x), 2, "e4m3")
    wt = f64(w_qkv).T
    q = xq @ mxq(wt[:, :C], 0, "e4m3")
    k = xq @ mxq(wt[:, C:2 * C], 0, "e4m3")
    v = xq @ mxq(wt[:, 2 * C:], 0, "e4m3")
    return rmsnorm(q, f64(q_norm_w)), rmsnorm(k, f64(k_norm_w)), v

@@ -1,0 +1,242 @@
+from contextlib import ExitStack
+
+import concourse.mybir as mybir
+from concourse.masks import make_identity
+
+F32 = mybir.dt.float32
+BF16 = mybir.dt.bfloat16
+U32 = mybir.dt.uint32
+U8 = mybir.dt.uint8
+I32 = mybir.dt.int32
+FP8X4 = mybir.dt.float8_e4m3fn_x4
+ALU = mybir.AluOpType
+ACT = mybir.ActivationFunctionType
+
+P = 128
+HIDDEN = 2048
+TOKENS = 256
+EPS = 1e-6
+PACK = 4
+K_PASS = P * PACK
+PASSES = HIDDEN // K_PASS
+WORDS_PER_PASS = K_PASS // 2
+ROWS_PER_PARTITION = 2
+UNIT = P * ROWS_PER_PARTITION
+TOKEN_TILES = TOKENS // P
+CHUNK = 512
+UNITS_PER_CHUNK = CHUNK // UNIT
+CHUNKS_PER_PART = HIDDEN // CHUNK
+PARTS = 3
+NORMED_PARTS = 2
+CHUNKS = PARTS * CHUNKS_PER_PART
+UNITS = CHUNKS * UNITS_PER_CHUNK
+CHUNKS_AHEAD = 3
+QUANTISE_LAG = 1
+MULTIPLY_LAG = 3
+TAKE_LAG = 4
+
+FLOPS = 2 * TOKENS * HIDDEN * PARTS * HIDDEN
+
+
+def as_multiplied(columns):
+    return columns.rearrange("m (h j p) -> m h p j", h=UNITS_PER_CHUNK, j=ROWS_PER_PARTITION)
+
+
+def as_stored(columns):
+    return columns.rearrange("m (h p j) -> m h p j", h=UNITS_PER_CHUNK, j=ROWS_PER_PARTITION)
+
+
+def tile_internattention_pa_kernel(tc, x, w_qkv, q_norm_w, k_norm_w, out_0, out_1, out_2):
+    nc = tc.nc
+    x_rows = x.flatten_outer_dims()
+    outs = [
+        out.flatten_outer_dims().rearrange("(p t) n -> p t n", t=TOKEN_TILES)
+        for out in (out_0, out_1, out_2)
+    ]
+    gain_vectors = [q_norm_w, k_norm_w]
+
+    with ExitStack() as ctx:
+        const = ctx.enter_context(tc.tile_pool(name="const", bufs=1))
+        raw_pool = ctx.enter_context(tc.tile_pool(name="raw", bufs=UNITS_PER_CHUNK * (CHUNKS_AHEAD + 1)))
+        grouped_pool = ctx.enter_context(tc.tile_pool(name="grouped", bufs=4))
+        codes_pool = ctx.enter_context(tc.tile_pool(name="codes", bufs=3))
+        normed_pool = ctx.enter_context(tc.tile_pool(name="normed", bufs=NORMED_PARTS * TOKEN_TILES))
+        plain_pool = ctx.enter_context(tc.tile_pool(name="plain", bufs=4))
+        squares_pool = ctx.enter_context(tc.tile_pool(name="squares", bufs=4))
+        stats_pool = ctx.enter_context(tc.tile_pool(name="stats", bufs=NORMED_PARTS))
+        bank_pool = ctx.enter_context(tc.psum_pool(name="bank", bufs=6))
+        acc_pool = ctx.enter_context(tc.psum_pool(name="acc", bufs=TOKEN_TILES))
+
+        identity = const.tile([P, P], F32)
+        make_identity(nc, identity[:])
+        x_codes = const.tile([P, PASSES, UNIT], U32, align_bytes=64)
+        x_scales = const.tile([P, PASSES, UNIT], U8, align_bytes=64)
+
+        gain_rows = [const.tile([P, HIDDEN], BF16, name="gain_row%d" % part) for part in range(NORMED_PARTS)]
+        gains = [const.tile([P, HIDDEN], BF16, name="gain%d" % part) for part in range(NORMED_PARTS)]
+        for part in range(NORMED_PARTS):
+            nc.vector.memset(gain_rows[part][:].bitcast(I32), 0)
+            nc.scalar.dma_start(out=gain_rows[part][0:1, :], in_=gain_vectors[part].unsqueeze(0))
+        all_ones = const.tile([P, P], BF16)
+        nc.vector.memset(all_ones[:], 1.0)
+
+        ones = const.tile([P, 1], F32)
+        nc.vector.memset(ones[:], 1.0)
+        warm = const.tile([P, 1], F32)
+        nc.scalar.sqrt(out=warm[:], in_=ones[:])
+
+        def spread_gain(part):
+            for i in range(CHUNKS_PER_PART):
+                columns = slice(i * CHUNK, (i + 1) * CHUNK)
+                bank = bank_pool.tile([P, 2, UNIT], F32)
+                row = bank[:].rearrange("p u r -> p (u r)")
+                nc.tensor.matmul(out=row, lhsT=all_ones[:], rhs=gain_rows[part][:, columns], start=True, stop=True)
+                if i % 2 == 0:
+                    nc.scalar.copy(out=gains[part][:, columns], in_=row)
+                else:
+                    nc.vector.tensor_copy(out=gains[part][:, columns], in_=row)
+
+        def load_unit(rows):
+            raw = raw_pool.tile([P, ROWS_PER_PARTITION, HIDDEN], BF16)
+            nc.sync.dma_start(out=raw[:], in_=rows.rearrange("(p j) k -> p j k", j=ROWS_PER_PARTITION))
+            return raw
+
+        def load_chunk(c):
+            first = c * CHUNK
+            return [load_unit(w_qkv[first + h * UNIT : first + (h + 1) * UNIT, :]) for h in range(UNITS_PER_CHUNK)]
+
+        def regroup_unit(raw, vector_helps):
+            grouped = grouped_pool.tile([P, PASSES, UNIT * PACK], BF16, align_bytes=64)
+            for g in range(PASSES):
+                bank = bank_pool.tile([P, 2, UNIT], F32)
+                for u in range(2):
+                    words = slice(g * WORDS_PER_PASS + u, (g + 1) * WORDS_PER_PASS, 2)
+                    for j in range(ROWS_PER_PARTITION):
+                        nc.tensor.transpose(
+                            bank[:, u, j * P : (j + 1) * P],
+                            raw[:, j, :].bitcast(F32)[:, words],
+                            identity[:],
+                        )
+                pairs = grouped[:, g, :].bitcast(F32).rearrange("p (r u) -> p r u", u=2)
+                if vector_helps and g == PASSES - 1:
+                    nc.vector.tensor_copy(out=pairs, in_=bank[:].rearrange("p u r -> p r u"))
+                else:
+                    nc.scalar.copy(out=pairs, in_=bank[:].rearrange("p u r -> p r u"))
+            return grouped
+
+        def quantise_unit(grouped, codes, scales, h):
+            columns = slice(h * UNIT, (h + 1) * UNIT)
+            for g in range(PASSES):
+                nc.vector.quantize_mx(
+                    out=codes[:, g, columns].bitcast(FP8X4),
+                    scales=scales[:, g, columns],
+                    in_=grouped[:, g, :],
+                )
+
+        def multiply(t, codes, scales):
+            acc = acc_pool.tile([P, CHUNK], F32)
+            for g in range(PASSES):
+                nc.tensor.matmul_mx(
+                    out=acc[:],
+                    lhsT=x_codes[:, g, t * P : (t + 1) * P].bitcast(FP8X4),
+                    lhsT_scale=x_scales[:, g, t * P : (t + 1) * P],
+                    rhs=codes[:, g, :].bitcast(FP8X4),
+                    rhs_scale=scales[:, g, :],
+                    start=(g == 0),
+                    stop=(g == PASSES - 1),
+                )
+            return acc
+
+        def take_normed(acc, t, part, i, sumsq, normed):
+            columns = slice(i * CHUNK, (i + 1) * CHUNK)
+            squares = squares_pool.tile([P, CHUNK], BF16)
+            nc.scalar.activation(out=squares[:], in_=acc[:], func=ACT.Square, accum_out=sumsq[:, t, i : i + 1])
+            nc.vector.tensor_tensor(
+                out=as_stored(normed[t][:, columns]),
+                in0=as_multiplied(acc[:]),
+                in1=as_stored(gains[part][:, columns]),
+                op=ALU.mult,
+            )
+
+        def take_plain(acc, t, i):
+            columns = slice(i * CHUNK, (i + 1) * CHUNK)
+            plain = plain_pool.tile([P, CHUNK], F32)
+            nc.scalar.copy(out=as_stored(plain[:]), in_=as_multiplied(acc[:]))
+            nc.sync.dma_start(out=outs[PARTS - 1][:, t, columns], in_=plain[:])
+
+        def root_mean_square(sumsq):
+            total = stats_pool.tile([P, TOKEN_TILES], F32)
+            nc.vector.tensor_reduce(out=total[:], in_=sumsq[:], axis=mybir.AxisListType.X, op=ALU.add)
+            mean = stats_pool.tile([P, TOKEN_TILES], F32)
+            nc.vector.tensor_scalar(
+                out=mean[:], in0=total[:], scalar1=1.0 / HIDDEN, scalar2=EPS, op0=ALU.mult, op1=ALU.add
+            )
+            rms = stats_pool.tile([P, TOKEN_TILES], F32)
+            nc.scalar.sqrt(out=rms[:], in_=mean[:])
+            return rms
+
+        def divide_and_store(t, part, rms, normed):
+            inverse = stats_pool.tile([P, 1], F32)
+            nc.vector.reciprocal(out=inverse[:], in_=rms[:, t : t + 1])
+            nc.vector.tensor_scalar_mul(out=normed[t][:], in0=normed[t][:], scalar1=inverse[:])
+            nc.sync.dma_start(out=outs[part][:, t, :], in_=normed[t][:])
+
+        ctx.enter_context(tc.manual_schedule())
+
+        x_raw = load_unit(x_rows)
+        raws = []
+        for c in range(CHUNKS_AHEAD):
+            raws.extend(load_chunk(c))
+
+        quantise_unit(regroup_unit(x_raw, True), x_codes, x_scales, 0)
+
+        regrouped = {}
+        operands = {}
+        accs = {}
+        sumsq = {}
+        normed = {}
+        rms = {}
+        for s in range(UNITS + TAKE_LAG):
+            if s % UNITS_PER_CHUNK == 0 and s // UNITS_PER_CHUNK + CHUNKS_AHEAD < CHUNKS:
+                raws.extend(load_chunk(s // UNITS_PER_CHUNK + CHUNKS_AHEAD))
+
+            unit = s - QUANTISE_LAG
+            if 0 <= unit < UNITS:
+                c = unit // UNITS_PER_CHUNK
+                if unit % UNITS_PER_CHUNK == 0:
+                    codes = codes_pool.tile([P, PASSES, CHUNK], U32, align_bytes=64)
+                    scales = codes_pool.tile([P, PASSES, CHUNK], U8, align_bytes=64)
+                    operands[c] = (codes, scales)
+                quantise_unit(regrouped[unit], *operands[c], unit % UNITS_PER_CHUNK)
+
+            job = s - TAKE_LAG
+            if 0 <= job < UNITS:
+                t = job % TOKEN_TILES
+                part = job // TOKEN_TILES // CHUNKS_PER_PART
+                i = job // TOKEN_TILES % CHUNKS_PER_PART
+                if part < NORMED_PARTS:
+                    if i == 0 and t == 0:
+                        sumsq[part] = stats_pool.tile([P, TOKEN_TILES, CHUNKS_PER_PART], F32, name="sumsq")
+                        normed[part] = [
+                            normed_pool.tile([P, HIDDEN], F32, name="normed") for each in range(TOKEN_TILES)
+                        ]
+                    take_normed(accs[job], t, part, i, sumsq[part], normed[part])
+                else:
+                    take_plain(accs[job], t, i)
+                if i == 0 and part > 0:
+                    divide_and_store(t, part - 1, rms[part - 1], normed[part - 1])
+
+            if s < UNITS:
+                regrouped[s] = regroup_unit(raws[s], s % 2 == 1 or s >= NORMED_PARTS * CHUNKS_PER_PART * UNITS_PER_CHUNK)
+
+            if 1 <= s <= NORMED_PARTS:
+                spread_gain(s - 1)
+            job = s - MULTIPLY_LAG
+            if 0 <= job < UNITS:
+                accs[job] = multiply(job % TOKEN_TILES, *operands[job // TOKEN_TILES])
+
+            job = s - TAKE_LAG
+            if job >= 0 and job % (TOKEN_TILES * CHUNKS_PER_PART) == TOKEN_TILES * CHUNKS_PER_PART - 1:
+                part = job // TOKEN_TILES // CHUNKS_PER_PART
+                if part < NORMED_PARTS:
+                    rms[part] = root_mean_square(sumsq[part])

@@ -19,8 +19,8 @@ EPS = 1e-6
 PACK = 4
 K_PASS = P * PACK
 PASSES = HIDDEN // K_PASS
-WORDS_PER_PASS = K_PASS // 2
 ROWS_PER_PARTITION = 2
+RUN = 16
 UNIT = P * ROWS_PER_PARTITION
 TOKEN_TILES = TOKENS // P
 CHUNK = 512
@@ -58,6 +58,7 @@ def tile_internattention_pa_kernel(tc, x, w_qkv, q_norm_w, k_norm_w, out_0, out_
     with ExitStack() as ctx:
         const = ctx.enter_context(tc.tile_pool(name="const", bufs=1))
         raw_pool = ctx.enter_context(tc.tile_pool(name="raw", bufs=UNITS_PER_CHUNK * (CHUNKS_AHEAD + 1)))
+        second_pool = ctx.enter_context(tc.tile_pool(name="second", bufs=3))
         grouped_pool = ctx.enter_context(tc.tile_pool(name="grouped", bufs=4))
         codes_pool = ctx.enter_context(tc.tile_pool(name="codes", bufs=3))
         normed_pool = ctx.enter_context(tc.tile_pool(name="normed", bufs=NORMED_PARTS * TOKEN_TILES))
@@ -72,13 +73,19 @@ def tile_internattention_pa_kernel(tc, x, w_qkv, q_norm_w, k_norm_w, out_0, out_
         x_codes = const.tile([P, PASSES, UNIT], U32, align_bytes=64)
         x_scales = const.tile([P, PASSES, UNIT], U8, align_bytes=64)
 
-        gain_rows = [const.tile([P, HIDDEN], BF16, name="gain_row%d" % part) for part in range(NORMED_PARTS)]
+        gain_rows = const.tile([P, CHUNK], BF16)
+        nc.vector.memset(gain_rows[:].bitcast(I32), 0)
         gains = [const.tile([P, HIDDEN], BF16, name="gain%d" % part) for part in range(NORMED_PARTS)]
-        for part in range(NORMED_PARTS):
-            nc.vector.memset(gain_rows[part][:].bitcast(I32), 0)
-            nc.scalar.dma_start(out=gain_rows[part][0:1, :], in_=gain_vectors[part].unsqueeze(0))
-        all_ones = const.tile([P, P], BF16)
-        nc.vector.memset(all_ones[:], 1.0)
+        selectors = const.tile([P, P], BF16)
+        nc.gpsimd.tensor_copy(out=selectors[:], in_=identity[:])
+
+        def load_gains():
+            for part in range(NORMED_PARTS):
+                first = part * CHUNKS_PER_PART
+                nc.sync.dma_start(
+                    out=gain_rows[first : first + CHUNKS_PER_PART, :],
+                    in_=gain_vectors[part].rearrange("(c n) -> c n", c=CHUNKS_PER_PART),
+                )
 
         ones = const.tile([P, 1], F32)
         nc.vector.memset(ones[:], 1.0)
@@ -86,15 +93,21 @@ def tile_internattention_pa_kernel(tc, x, w_qkv, q_norm_w, k_norm_w, out_0, out_
         nc.scalar.sqrt(out=warm[:], in_=ones[:])
 
         def spread_gain(part):
-            for i in range(CHUNKS_PER_PART):
-                columns = slice(i * CHUNK, (i + 1) * CHUNK)
-                bank = bank_pool.tile([P, 2, UNIT], F32)
-                row = bank[:].rearrange("p u r -> p (u r)")
-                nc.tensor.matmul(out=row, lhsT=all_ones[:], rhs=gain_rows[part][:, columns], start=True, stop=True)
-                if i % 2 == 0:
-                    nc.scalar.copy(out=gains[part][:, columns], in_=row)
-                else:
-                    nc.vector.tensor_copy(out=gains[part][:, columns], in_=row)
+            for half in range(2):
+                bank = bank_pool.tile([P, 2, CHUNK], BF16)
+                for i in range(2):
+                    row = part * CHUNKS_PER_PART + half * 2 + i
+                    nc.tensor.matmul(
+                        out=bank[:, i, :],
+                        lhsT=selectors[:, row : row + 1].to_broadcast([P, P]),
+                        rhs=gain_rows[:],
+                        start=True,
+                        stop=True,
+                    )
+                nc.scalar.copy(
+                    out=gains[part][:, half * 2 * CHUNK : (half + 1) * 2 * CHUNK],
+                    in_=bank[:].rearrange("p i n -> p (i n)"),
+                )
 
         def load_unit(rows):
             raw = raw_pool.tile([P, ROWS_PER_PARTITION, HIDDEN], BF16)
@@ -105,16 +118,24 @@ def tile_internattention_pa_kernel(tc, x, w_qkv, q_norm_w, k_norm_w, out_0, out_
             first = c * CHUNK
             return [load_unit(w_qkv[first + h * UNIT : first + (h + 1) * UNIT, :]) for h in range(UNITS_PER_CHUNK)]
 
-        def regroup_unit(raw, vector_helps):
+        def order_unit(raw):
+            second = second_pool.tile([P, ROWS_PER_PARTITION, HIDDEN // 2], BF16)
+            runs = raw[:].rearrange("p j (h r q w) -> p j h r q w", h=2, q=2, w=RUN)
+            seconds = second[:].rearrange("p j (r h w) -> p j h r w", h=2, w=RUN)
+            for h in range(2):
+                nc.vector.tensor_copy(out=seconds[:, :, h], in_=runs[:, :, h, :, 1])
+            nc.vector.tensor_copy(out=runs[:, :, 0, :, 1], in_=runs[:, :, 1, :, 0])
+            return raw, second
+
+        def regroup_unit(ordered, vector_helps):
             grouped = grouped_pool.tile([P, PASSES, UNIT * PACK], BF16, align_bytes=64)
             for g in range(PASSES):
                 bank = bank_pool.tile([P, 2, UNIT], F32)
                 for u in range(2):
-                    words = slice(g * WORDS_PER_PASS + u, (g + 1) * WORDS_PER_PASS, 2)
                     for j in range(ROWS_PER_PARTITION):
                         nc.tensor.transpose(
                             bank[:, u, j * P : (j + 1) * P],
-                            raw[:, j, :].bitcast(F32)[:, words],
+                            ordered[u][:, j, :].bitcast(F32)[:, g * P : (g + 1) * P],
                             identity[:],
                         )
                 pairs = grouped[:, g, :].bitcast(F32).rearrange("p (r u) -> p r u", u=2)
@@ -175,20 +196,33 @@ def tile_internattention_pa_kernel(tc, x, w_qkv, q_norm_w, k_norm_w, out_0, out_
             nc.scalar.sqrt(out=rms[:], in_=mean[:])
             return rms
 
-        def divide_and_store(t, part, rms, normed):
-            inverse = stats_pool.tile([P, 1], F32)
-            nc.vector.reciprocal(out=inverse[:], in_=rms[:, t : t + 1])
-            nc.vector.tensor_scalar_mul(out=normed[t][:], in0=normed[t][:], scalar1=inverse[:])
-            nc.sync.dma_start(out=outs[part][:, t, :], in_=normed[t][:])
+        def invert(rms):
+            inverse = stats_pool.tile([P, TOKEN_TILES], F32)
+            nc.vector.reciprocal(out=inverse[:], in_=rms[:])
+            return inverse
+
+        def divide(part, i, inverse, normed):
+            columns = slice(i * CHUNK, (i + 1) * CHUNK)
+            nc.scalar.activation(
+                out=normed[0][:, columns], in_=normed[0][:, columns], func=ACT.Copy, scale=inverse[:, 0:1]
+            )
+            nc.vector.tensor_scalar_mul(out=normed[1][:, columns], in0=normed[1][:, columns], scalar1=inverse[:, 1:2])
+            if i % 2 == 1:
+                columns = slice((i - 1) * CHUNK, (i + 1) * CHUNK)
+                for t in range(TOKEN_TILES):
+                    nc.sync.dma_start(out=outs[part][:, t, columns], in_=normed[t][:, columns])
 
         ctx.enter_context(tc.manual_schedule())
 
         x_raw = load_unit(x_rows)
+        load_gains()
         raws = []
         for c in range(CHUNKS_AHEAD):
             raws.extend(load_chunk(c))
 
-        quantise_unit(regroup_unit(x_raw, True), x_codes, x_scales, 0)
+        x_ordered = order_unit(x_raw)
+        ordered = {0: order_unit(raws[0])}
+        quantise_unit(regroup_unit(x_ordered, False), x_codes, x_scales, 0)
 
         regrouped = {}
         operands = {}
@@ -196,10 +230,13 @@ def tile_internattention_pa_kernel(tc, x, w_qkv, q_norm_w, k_norm_w, out_0, out_
         sumsq = {}
         normed = {}
         rms = {}
+        inverse = {}
         for s in range(UNITS + TAKE_LAG):
             if s % UNITS_PER_CHUNK == 0 and s // UNITS_PER_CHUNK + CHUNKS_AHEAD < CHUNKS:
                 raws.extend(load_chunk(s // UNITS_PER_CHUNK + CHUNKS_AHEAD))
 
+            if s + 1 < UNITS:
+                ordered[s + 1] = order_unit(raws[s + 1])
             unit = s - QUANTISE_LAG
             if 0 <= unit < UNITS:
                 c = unit // UNITS_PER_CHUNK
@@ -223,11 +260,14 @@ def tile_internattention_pa_kernel(tc, x, w_qkv, q_norm_w, k_norm_w, out_0, out_
                     take_normed(accs[job], t, part, i, sumsq[part], normed[part])
                 else:
                     take_plain(accs[job], t, i)
-                if i == 0 and part > 0:
-                    divide_and_store(t, part - 1, rms[part - 1], normed[part - 1])
+                n = job % (TOKEN_TILES * CHUNKS_PER_PART)
+                if part > 0 and n == 0:
+                    inverse[part - 1] = invert(rms[part - 1])
+                if part > 0 and 1 <= n <= CHUNKS_PER_PART:
+                    divide(part - 1, n - 1, inverse[part - 1], normed[part - 1])
 
             if s < UNITS:
-                regrouped[s] = regroup_unit(raws[s], s % 2 == 1 or s >= NORMED_PARTS * CHUNKS_PER_PART * UNITS_PER_CHUNK)
+                regrouped[s] = regroup_unit(ordered[s], s % 2 == 1 and s >= NORMED_PARTS * CHUNKS_PER_PART * UNITS_PER_CHUNK)
 
             if 1 <= s <= NORMED_PARTS:
                 spread_gain(s - 1)

@@ -203,10 +203,10 @@ def tile_internattention_pa_kernel(tc, x, w_qkv, q_norm_w, k_norm_w, out_0, out_
 
         def divide(part, i, inverse, normed):
             columns = slice(i * CHUNK, (i + 1) * CHUNK)
-            nc.scalar.activation(
-                out=normed[0][:, columns], in_=normed[0][:, columns], func=ACT.Copy, scale=inverse[:, 0:1]
-            )
-            nc.vector.tensor_scalar_mul(out=normed[1][:, columns], in0=normed[1][:, columns], scalar1=inverse[:, 1:2])
+            for t in range(TOKEN_TILES):
+                nc.vector.tensor_scalar_mul(
+                    out=normed[t][:, columns], in0=normed[t][:, columns], scalar1=inverse[:, t : t + 1]
+                )
             if i % 2 == 1:
                 columns = slice((i - 1) * CHUNK, (i + 1) * CHUNK)
                 for t in range(TOKEN_TILES):
@@ -267,7 +267,7 @@ def tile_internattention_pa_kernel(tc, x, w_qkv, q_norm_w, k_norm_w, out_0, out_
                     divide(part - 1, n - 1, inverse[part - 1], normed[part - 1])
 
             if s < UNITS:
-                regrouped[s] = regroup_unit(ordered[s], s % 2 == 1 and s >= NORMED_PARTS * CHUNKS_PER_PART * UNITS_PER_CHUNK)
+                regrouped[s] = regroup_unit(ordered[s], s >= NORMED_PARTS * CHUNKS_PER_PART * UNITS_PER_CHUNK)
 
             if 1 <= s <= NORMED_PARTS:
                 spread_gain(s - 1)

@@ -19,31 +19,35 @@ EPS = 1e-6
 PACK = 4
 K_PASS = P * PACK
 PASSES = HIDDEN // K_PASS
-ROWS_PER_PARTITION = 2
+PLAIN_PASSES = 1
+PLAIN_K = PLAIN_PASSES * K_PASS
+SORTED_K = HIDDEN - PLAIN_K
 RUN = 16
-UNIT = P * ROWS_PER_PARTITION
 TOKEN_TILES = TOKENS // P
 CHUNK = 512
-UNITS_PER_CHUNK = CHUNK // UNIT
+ROWS = CHUNK // P
+BANK_ROWS = 2
 CHUNKS_PER_PART = HIDDEN // CHUNK
 PARTS = 3
 NORMED_PARTS = 2
 CHUNKS = PARTS * CHUNKS_PER_PART
-UNITS = CHUNKS * UNITS_PER_CHUNK
+STEPS_PER_CHUNK = 2
+STEP_PASSES = PASSES // STEPS_PER_CHUNK
+STEPS = CHUNKS * STEPS_PER_CHUNK
 CHUNKS_AHEAD = 3
-QUANTISE_LAG = 1
-MULTIPLY_LAG = 3
-TAKE_LAG = 4
+QUANTISE_LAG = 2
+MULTIPLY_LAG = 4
+TAKE_LAG = 5
 
 FLOPS = 2 * TOKENS * HIDDEN * PARTS * HIDDEN
 
 
 def as_multiplied(columns):
-    return columns.rearrange("m (h j p) -> m h p j", h=UNITS_PER_CHUNK, j=ROWS_PER_PARTITION)
+    return columns.rearrange("m (j p) -> m p j", j=ROWS)
 
 
 def as_stored(columns):
-    return columns.rearrange("m (h p j) -> m h p j", h=UNITS_PER_CHUNK, j=ROWS_PER_PARTITION)
+    return columns.rearrange("m (p j) -> m p j", j=ROWS)
 
 
 def tile_internattention_pa_kernel(tc, x, w_qkv, q_norm_w, k_norm_w, out_0, out_1, out_2):
@@ -57,10 +61,10 @@ def tile_internattention_pa_kernel(tc, x, w_qkv, q_norm_w, k_norm_w, out_0, out_
 
     with ExitStack() as ctx:
         const = ctx.enter_context(tc.tile_pool(name="const", bufs=1))
-        raw_pool = ctx.enter_context(tc.tile_pool(name="raw", bufs=UNITS_PER_CHUNK * (CHUNKS_AHEAD + 1)))
-        second_pool = ctx.enter_context(tc.tile_pool(name="second", bufs=3))
-        grouped_pool = ctx.enter_context(tc.tile_pool(name="grouped", bufs=4))
-        codes_pool = ctx.enter_context(tc.tile_pool(name="codes", bufs=3))
+        raw_pool = ctx.enter_context(tc.tile_pool(name="raw", bufs=CHUNKS_AHEAD + 1))
+        second_pool = ctx.enter_context(tc.tile_pool(name="second", bufs=2))
+        grouped_pool = ctx.enter_context(tc.tile_pool(name="grouped", bufs=5))
+        codes_pool = ctx.enter_context(tc.tile_pool(name="codes", bufs=4))
         normed_pool = ctx.enter_context(tc.tile_pool(name="normed", bufs=NORMED_PARTS * TOKEN_TILES))
         plain_pool = ctx.enter_context(tc.tile_pool(name="plain", bufs=4))
         squares_pool = ctx.enter_context(tc.tile_pool(name="squares", bufs=4))
@@ -70,8 +74,10 @@ def tile_internattention_pa_kernel(tc, x, w_qkv, q_norm_w, k_norm_w, out_0, out_
 
         identity = const.tile([P, P], F32)
         make_identity(nc, identity[:])
-        x_codes = const.tile([P, PASSES, UNIT], U32, align_bytes=64)
-        x_scales = const.tile([P, PASSES, UNIT], U8, align_bytes=64)
+        x_raw = const.tile([P, TOKEN_TILES, HIDDEN], BF16)
+        x_second = const.tile([P, TOKEN_TILES, SORTED_K // 2], BF16)
+        x_codes = const.tile([P, PASSES, TOKENS], U32, align_bytes=64)
+        x_scales = const.tile([P, PASSES, TOKENS], U8, align_bytes=64)
 
         gain_rows = const.tile([P, CHUNK], BF16)
         nc.vector.memset(gain_rows[:].bitcast(I32), 0)
@@ -87,10 +93,8 @@ def tile_internattention_pa_kernel(tc, x, w_qkv, q_norm_w, k_norm_w, out_0, out_
                     in_=gain_vectors[part].rearrange("(c n) -> c n", c=CHUNKS_PER_PART),
                 )
 
-        ones = const.tile([P, 1], F32)
-        nc.vector.memset(ones[:], 1.0)
-        warm = const.tile([P, 1], F32)
-        nc.scalar.sqrt(out=warm[:], in_=ones[:])
+        minus_half = const.tile([P, TOKEN_TILES, 1], F32)
+        nc.gpsimd.memset(minus_half[:], -0.5)
 
         def spread_gain(part):
             for half in range(2):
@@ -104,55 +108,55 @@ def tile_internattention_pa_kernel(tc, x, w_qkv, q_norm_w, k_norm_w, out_0, out_
                         start=True,
                         stop=True,
                     )
-                nc.scalar.copy(
+                nc.vector.tensor_copy(
                     out=gains[part][:, half * 2 * CHUNK : (half + 1) * 2 * CHUNK],
                     in_=bank[:].rearrange("p i n -> p (i n)"),
                 )
 
-        def load_unit(rows):
-            raw = raw_pool.tile([P, ROWS_PER_PARTITION, HIDDEN], BF16)
-            nc.sync.dma_start(out=raw[:], in_=rows.rearrange("(p j) k -> p j k", j=ROWS_PER_PARTITION))
+        def load_chunk(c):
+            raw = raw_pool.tile([P, ROWS, HIDDEN], BF16)
+            rows = w_qkv[c * CHUNK : (c + 1) * CHUNK, :].rearrange("(p j) k -> p j k", j=ROWS)
+            for first in range(0, ROWS, BANK_ROWS):
+                here = slice(first, first + BANK_ROWS)
+                nc.sync.dma_start(out=raw[:, here, :], in_=rows[:, here, :])
             return raw
 
-        def load_chunk(c):
-            first = c * CHUNK
-            return [load_unit(w_qkv[first + h * UNIT : first + (h + 1) * UNIT, :]) for h in range(UNITS_PER_CHUNK)]
-
-        def order_unit(raw):
-            second = second_pool.tile([P, ROWS_PER_PARTITION, HIDDEN // 2], BF16)
-            runs = raw[:].rearrange("p j (h r q w) -> p j h r q w", h=2, q=2, w=RUN)
-            seconds = second[:].rearrange("p j (r h w) -> p j h r w", h=2, w=RUN)
+        def sort_rows(raw, second):
+            runs = raw[:, :, PLAIN_K:].rearrange("p j (h r q w) -> p j h r q w", h=2, q=2, w=RUN)
+            seconds = second.rearrange("p j (r h w) -> p j h r w", h=2, w=RUN)
             for h in range(2):
                 nc.vector.tensor_copy(out=seconds[:, :, h], in_=runs[:, :, h, :, 1])
             nc.vector.tensor_copy(out=runs[:, :, 0, :, 1], in_=runs[:, :, 1, :, 0])
+
+        def sort_chunk(raw):
+            second = second_pool.tile([P, ROWS, SORTED_K // 2], BF16)
+            sort_rows(raw[:], second[:])
             return raw, second
 
-        def regroup_unit(ordered, vector_helps):
-            grouped = grouped_pool.tile([P, PASSES, UNIT * PACK], BF16, align_bytes=64)
-            for g in range(PASSES):
-                bank = bank_pool.tile([P, 2, UNIT], F32)
-                for u in range(2):
-                    for j in range(ROWS_PER_PARTITION):
-                        nc.tensor.transpose(
-                            bank[:, u, j * P : (j + 1) * P],
-                            ordered[u][:, j, :].bitcast(F32)[:, g * P : (g + 1) * P],
-                            identity[:],
-                        )
-                pairs = grouped[:, g, :].bitcast(F32).rearrange("p (r u) -> p r u", u=2)
-                if vector_helps and g == PASSES - 1:
-                    nc.vector.tensor_copy(out=pairs, in_=bank[:].rearrange("p u r -> p r u"))
-                else:
-                    nc.scalar.copy(out=pairs, in_=bank[:].rearrange("p u r -> p r u"))
-            return grouped
+        def regroup(raw, second, g, first_row, target, on_vector):
+            bank = bank_pool.tile([P, 2, BANK_ROWS * P], F32)
+            for u in range(2):
+                for j in range(BANK_ROWS):
+                    row = first_row + j
+                    if g < PLAIN_PASSES:
+                        words = raw[:, row, g * K_PASS : (g + 1) * K_PASS].bitcast(F32)[:, u::2]
+                    else:
+                        half = (raw[:, row, PLAIN_K:], second[:, row, :])[u].bitcast(F32)
+                        words = half[:, (g - PLAIN_PASSES) * P : (g - PLAIN_PASSES + 1) * P]
+                    nc.tensor.transpose(bank[:, u, j * P : (j + 1) * P], words, identity[:])
+            copy = nc.vector.tensor_copy if on_vector else nc.scalar.copy
+            copy(
+                out=target.bitcast(F32).rearrange("p (r u) -> p r u", u=2),
+                in_=bank[:].rearrange("p u r -> p r u"),
+            )
 
-        def quantise_unit(grouped, codes, scales, h):
-            columns = slice(h * UNIT, (h + 1) * UNIT)
-            for g in range(PASSES):
-                nc.vector.quantize_mx(
-                    out=codes[:, g, columns].bitcast(FP8X4),
-                    scales=scales[:, g, columns],
-                    in_=grouped[:, g, :],
-                )
+        def quantise(grouped, codes, scales, passes):
+            here = slice(passes[0], passes[-1] + 1)
+            nc.vector.quantize_mx(
+                out=codes[:, here, :].rearrange("p g n -> p (g n)").bitcast(FP8X4),
+                scales=scales[:, here, :].rearrange("p g n -> p (g n)"),
+                in_=grouped,
+            )
 
         def multiply(t, codes, scales):
             acc = acc_pool.tile([P, CHUNK], F32)
@@ -182,72 +186,91 @@ def tile_internattention_pa_kernel(tc, x, w_qkv, q_norm_w, k_norm_w, out_0, out_
         def take_plain(acc, t, i):
             columns = slice(i * CHUNK, (i + 1) * CHUNK)
             plain = plain_pool.tile([P, CHUNK], F32)
-            nc.scalar.copy(out=as_stored(plain[:]), in_=as_multiplied(acc[:]))
+            copy = nc.vector.tensor_copy if i == CHUNKS_PER_PART - 1 and t == 1 else nc.scalar.copy
+            copy(out=as_stored(plain[:]), in_=as_multiplied(acc[:]))
             nc.sync.dma_start(out=outs[PARTS - 1][:, t, columns], in_=plain[:])
 
-        def root_mean_square(sumsq):
-            total = stats_pool.tile([P, TOKEN_TILES], F32)
-            nc.vector.tensor_reduce(out=total[:], in_=sumsq[:], axis=mybir.AxisListType.X, op=ALU.add)
-            mean = stats_pool.tile([P, TOKEN_TILES], F32)
-            nc.vector.tensor_scalar(
+        def invert_root_mean_square(sumsq):
+            pairs = stats_pool.tile([P, TOKEN_TILES, 2], F32)
+            nc.gpsimd.tensor_tensor(out=pairs[:], in0=sumsq[:, :, 0:2], in1=sumsq[:, :, 2:4], op=ALU.add)
+            total = stats_pool.tile([P, TOKEN_TILES, 1], F32)
+            nc.gpsimd.tensor_tensor(out=total[:], in0=pairs[:, :, 0:1], in1=pairs[:, :, 1:2], op=ALU.add)
+            mean = stats_pool.tile([P, TOKEN_TILES, 1], F32)
+            nc.gpsimd.tensor_scalar(
                 out=mean[:], in0=total[:], scalar1=1.0 / HIDDEN, scalar2=EPS, op0=ALU.mult, op1=ALU.add
             )
-            rms = stats_pool.tile([P, TOKEN_TILES], F32)
-            nc.scalar.sqrt(out=rms[:], in_=mean[:])
-            return rms
-
-        def invert(rms):
-            inverse = stats_pool.tile([P, TOKEN_TILES], F32)
-            nc.vector.reciprocal(out=inverse[:], in_=rms[:])
+            inverse = stats_pool.tile([P, TOKEN_TILES, 1], F32)
+            nc.gpsimd.tensor_tensor(out=inverse[:], in0=mean[:], in1=minus_half[:], op=ALU.pow)
             return inverse
 
-        def divide(part, i, inverse, normed):
-            columns = slice(i * CHUNK, (i + 1) * CHUNK)
+        def divide(part, half, inverse, normed):
+            columns = slice(half * HIDDEN // 2, (half + 1) * HIDDEN // 2)
             for t in range(TOKEN_TILES):
                 nc.vector.tensor_scalar_mul(
-                    out=normed[t][:, columns], in0=normed[t][:, columns], scalar1=inverse[:, t : t + 1]
+                    out=normed[t][:, columns], in0=normed[t][:, columns], scalar1=inverse[:, t, :]
                 )
-            if i % 2 == 1:
-                columns = slice((i - 1) * CHUNK, (i + 1) * CHUNK)
-                for t in range(TOKEN_TILES):
-                    nc.sync.dma_start(out=outs[part][:, t, columns], in_=normed[t][:, columns])
+                nc.sync.dma_start(out=outs[part][:, t, columns], in_=normed[t][:, columns])
 
         ctx.enter_context(tc.manual_schedule())
 
-        x_raw = load_unit(x_rows)
+        nc.sync.dma_start(out=x_raw[:], in_=x_rows.rearrange("(p j) k -> p j k", j=TOKEN_TILES))
+        raws = [load_chunk(0)]
         load_gains()
-        raws = []
-        for c in range(CHUNKS_AHEAD):
-            raws.extend(load_chunk(c))
+        for c in range(1, CHUNKS_AHEAD):
+            raws.append(load_chunk(c))
 
-        x_ordered = order_unit(x_raw)
-        ordered = {0: order_unit(raws[0])}
-        quantise_unit(regroup_unit(x_ordered, False), x_codes, x_scales, 0)
+        sort_rows(x_raw[:], x_second[:])
+        passes = list(range(PASSES))
+        x_grouped = const.tile([P, PASSES, TOKENS * PACK], BF16, align_bytes=64)
+        for g in passes:
+            regroup(x_raw, x_second, g, 0, x_grouped[:, g, :], g % 2 == 1)
+        ordered = {}
+        ordered[0] = (raws[0], second_pool.tile([P, ROWS, SORTED_K // 2], BF16, name="second"))
+        for first in range(0, ROWS, BANK_ROWS):
+            here = slice(first, first + BANK_ROWS)
+            sort_rows(ordered[0][0][:, here, :], ordered[0][1][:, here, :])
+            if first == 0:
+                quantise(x_grouped[:].rearrange("p g c -> p (g c)"), x_codes, x_scales, passes)
 
-        regrouped = {}
+        def passes_of(s):
+            first = s % STEPS_PER_CHUNK * STEP_PASSES
+            return list(range(first, first + STEP_PASSES))
+
+        def banks_of(s):
+            if s < STEPS_PER_CHUNK:
+                return [(g, s * BANK_ROWS) for g in range(PASSES)]
+            return [(g, first) for g in passes_of(s) for first in range(0, ROWS, BANK_ROWS)]
+
+        def vector_banks(s):
+            return (1, 3) if s == STEPS - 1 else ()
+
+        grouped = {}
         operands = {}
         accs = {}
         sumsq = {}
         normed = {}
-        rms = {}
         inverse = {}
-        for s in range(UNITS + TAKE_LAG):
-            if s % UNITS_PER_CHUNK == 0 and s // UNITS_PER_CHUNK + CHUNKS_AHEAD < CHUNKS:
-                raws.extend(load_chunk(s // UNITS_PER_CHUNK + CHUNKS_AHEAD))
+        for s in range(STEPS + TAKE_LAG):
+            c = s // STEPS_PER_CHUNK
+            if s % STEPS_PER_CHUNK == 0 and c + CHUNKS_AHEAD < CHUNKS:
+                raws.append(load_chunk(c + CHUNKS_AHEAD))
 
-            if s + 1 < UNITS:
-                ordered[s + 1] = order_unit(raws[s + 1])
-            unit = s - QUANTISE_LAG
-            if 0 <= unit < UNITS:
-                c = unit // UNITS_PER_CHUNK
-                if unit % UNITS_PER_CHUNK == 0:
+            done = s - QUANTISE_LAG
+            if 0 <= done < STEPS:
+                c = done // STEPS_PER_CHUNK
+                if done % STEPS_PER_CHUNK == 0:
                     codes = codes_pool.tile([P, PASSES, CHUNK], U32, align_bytes=64)
                     scales = codes_pool.tile([P, PASSES, CHUNK], U8, align_bytes=64)
                     operands[c] = (codes, scales)
-                quantise_unit(regrouped[unit], *operands[c], unit % UNITS_PER_CHUNK)
+                half = grouped[c, done % STEPS_PER_CHUNK]
+                if done < STEPS - 1:
+                    quantise(half[:].rearrange("p g c -> p (g c)"), *operands[c], passes_of(done))
+                else:
+                    for i in range(STEP_PASSES):
+                        quantise(half[:, i, :], *operands[c], passes_of(done)[i : i + 1])
 
             job = s - TAKE_LAG
-            if 0 <= job < UNITS:
+            if 0 <= job < STEPS:
                 t = job % TOKEN_TILES
                 part = job // TOKEN_TILES // CHUNKS_PER_PART
                 i = job // TOKEN_TILES % CHUNKS_PER_PART
@@ -258,25 +281,30 @@ def tile_internattention_pa_kernel(tc, x, w_qkv, q_norm_w, k_norm_w, out_0, out_
                             normed_pool.tile([P, HIDDEN], F32, name="normed") for each in range(TOKEN_TILES)
                         ]
                     take_normed(accs[job], t, part, i, sumsq[part], normed[part])
+                    if job % (TOKEN_TILES * CHUNKS_PER_PART) == TOKEN_TILES * CHUNKS_PER_PART - 1:
+                        inverse[part] = invert_root_mean_square(sumsq[part])
                 else:
                     take_plain(accs[job], t, i)
                 n = job % (TOKEN_TILES * CHUNKS_PER_PART)
-                if part > 0 and n == 0:
-                    inverse[part - 1] = invert(rms[part - 1])
-                if part > 0 and 1 <= n <= CHUNKS_PER_PART:
+                if part > 0 and 1 <= n <= 2:
                     divide(part - 1, n - 1, inverse[part - 1], normed[part - 1])
 
-            if s < UNITS:
-                regrouped[s] = regroup_unit(ordered[s], s >= NORMED_PARTS * CHUNKS_PER_PART * UNITS_PER_CHUNK)
+            c = s // STEPS_PER_CHUNK
+            if s < STEPS:
+                for n, (g, first) in enumerate(banks_of(s)):
+                    half = (c, g // STEP_PASSES)
+                    if half not in grouped:
+                        grouped[half] = grouped_pool.tile(
+                            [P, STEP_PASSES, CHUNK * PACK], BF16, align_bytes=64, name="grouped"
+                        )
+                    target = grouped[half][:, g % STEP_PASSES, first * P * PACK : (first + BANK_ROWS) * P * PACK]
+                    regroup(*ordered[c], g, first, target, n in vector_banks(s))
 
             if 1 <= s <= NORMED_PARTS:
                 spread_gain(s - 1)
-            job = s - MULTIPLY_LAG
-            if 0 <= job < UNITS:
-                accs[job] = multiply(job % TOKEN_TILES, *operands[job // TOKEN_TILES])
+            if s % STEPS_PER_CHUNK == 0 and c + 1 < CHUNKS:
+                ordered[c + 1] = sort_chunk(raws[c + 1])
 
-            job = s - TAKE_LAG
-            if job >= 0 and job % (TOKEN_TILES * CHUNKS_PER_PART) == TOKEN_TILES * CHUNKS_PER_PART - 1:
-                part = job // TOKEN_TILES // CHUNKS_PER_PART
-                if part < NORMED_PARTS:
-                    rms[part] = root_mean_square(sumsq[part])
+            job = s - MULTIPLY_LAG
+            if 0 <= job < STEPS:
+                accs[job] = multiply(job % TOKEN_TILES, *operands[job // TOKEN_TILES])

@@ -25,16 +25,17 @@ SORTED_K = HIDDEN - PLAIN_K
 RUN = 16
 TOKEN_TILES = TOKENS // P
 CHUNK = 512
-ROWS = CHUNK // P
-BANK_ROWS = 2
+BLOCK = 256
+BLOCK_ROWS = BLOCK // P
+BLOCKS = CHUNK // BLOCK
 CHUNKS_PER_PART = HIDDEN // CHUNK
 PARTS = 3
 NORMED_PARTS = 2
 CHUNKS = PARTS * CHUNKS_PER_PART
-STEPS_PER_CHUNK = 2
-STEP_PASSES = PASSES // STEPS_PER_CHUNK
-STEPS = CHUNKS * STEPS_PER_CHUNK
-CHUNKS_AHEAD = 3
+STEPS = CHUNKS * BLOCKS
+SORT_LEAD = 2
+BLOCKS_AHEAD = 9
+PASSES_AT_ONCE = PASSES // BLOCKS
 QUANTISE_LAG = 2
 MULTIPLY_LAG = 4
 TAKE_LAG = 5
@@ -43,11 +44,11 @@ FLOPS = 2 * TOKENS * HIDDEN * PARTS * HIDDEN
 
 
 def as_multiplied(columns):
-    return columns.rearrange("m (j p) -> m p j", j=ROWS)
+    return columns.rearrange("m (h j p) -> m h p j", j=BLOCK_ROWS, p=P)
 
 
 def as_stored(columns):
-    return columns.rearrange("m (p j) -> m p j", j=ROWS)
+    return columns.rearrange("m (h p j) -> m h p j", j=BLOCK_ROWS, p=P)
 
 
 def tile_internattention_pa_kernel(tc, x, w_qkv, q_norm_w, k_norm_w, out_0, out_1, out_2):
@@ -61,21 +62,19 @@ def tile_internattention_pa_kernel(tc, x, w_qkv, q_norm_w, k_norm_w, out_0, out_
 
     with ExitStack() as ctx:
         const = ctx.enter_context(tc.tile_pool(name="const", bufs=1))
-        raw_pool = ctx.enter_context(tc.tile_pool(name="raw", bufs=CHUNKS_AHEAD + 1))
-        second_pool = ctx.enter_context(tc.tile_pool(name="second", bufs=2))
+        raw_pool = ctx.enter_context(tc.tile_pool(name="raw", bufs=BLOCKS_AHEAD + 1))
+        second_pool = ctx.enter_context(tc.tile_pool(name="second", bufs=4))
         grouped_pool = ctx.enter_context(tc.tile_pool(name="grouped", bufs=5))
-        codes_pool = ctx.enter_context(tc.tile_pool(name="codes", bufs=4))
+        codes_pool = ctx.enter_context(tc.tile_pool(name="codes", bufs=3))
         normed_pool = ctx.enter_context(tc.tile_pool(name="normed", bufs=NORMED_PARTS * TOKEN_TILES))
-        plain_pool = ctx.enter_context(tc.tile_pool(name="plain", bufs=4))
-        squares_pool = ctx.enter_context(tc.tile_pool(name="squares", bufs=4))
+        plain_pool = ctx.enter_context(tc.tile_pool(name="plain", bufs=6))
+        squares_pool = ctx.enter_context(tc.tile_pool(name="squares", bufs=2))
         stats_pool = ctx.enter_context(tc.tile_pool(name="stats", bufs=NORMED_PARTS))
         bank_pool = ctx.enter_context(tc.psum_pool(name="bank", bufs=6))
         acc_pool = ctx.enter_context(tc.psum_pool(name="acc", bufs=TOKEN_TILES))
 
         identity = const.tile([P, P], F32)
         make_identity(nc, identity[:])
-        x_raw = const.tile([P, TOKEN_TILES, HIDDEN], BF16)
-        x_second = const.tile([P, TOKEN_TILES, SORTED_K // 2], BF16)
         x_codes = const.tile([P, PASSES, TOKENS], U32, align_bytes=64)
         x_scales = const.tile([P, PASSES, TOKENS], U8, align_bytes=64)
 
@@ -113,38 +112,33 @@ def tile_internattention_pa_kernel(tc, x, w_qkv, q_norm_w, k_norm_w, out_0, out_
                     in_=bank[:].rearrange("p i n -> p (i n)"),
                 )
 
-        def load_chunk(c):
-            raw = raw_pool.tile([P, ROWS, HIDDEN], BF16)
-            rows = w_qkv[c * CHUNK : (c + 1) * CHUNK, :].rearrange("(p j) k -> p j k", j=ROWS)
-            for first in range(0, ROWS, BANK_ROWS):
-                here = slice(first, first + BANK_ROWS)
-                nc.sync.dma_start(out=raw[:, here, :], in_=rows[:, here, :])
+        def load_block(rows):
+            raw = raw_pool.tile([P, BLOCK_ROWS, HIDDEN], BF16)
+            nc.sync.dma_start(out=raw[:], in_=rows.rearrange("(p j) k -> p j k", j=BLOCK_ROWS))
             return raw
 
-        def sort_rows(raw, second):
+        def load_weights(s):
+            return load_block(w_qkv[s * BLOCK : (s + 1) * BLOCK, :])
+
+        def sort_block(raw):
+            second = second_pool.tile([P, BLOCK_ROWS, SORTED_K // 2], BF16)
             runs = raw[:, :, PLAIN_K:].rearrange("p j (h r q w) -> p j h r q w", h=2, q=2, w=RUN)
-            seconds = second.rearrange("p j (r h w) -> p j h r w", h=2, w=RUN)
+            seconds = second[:].rearrange("p j (r h w) -> p j h r w", h=2, w=RUN)
             for h in range(2):
                 nc.vector.tensor_copy(out=seconds[:, :, h], in_=runs[:, :, h, :, 1])
             nc.vector.tensor_copy(out=runs[:, :, 0, :, 1], in_=runs[:, :, 1, :, 0])
-
-        def sort_chunk(raw):
-            second = second_pool.tile([P, ROWS, SORTED_K // 2], BF16)
-            sort_rows(raw[:], second[:])
             return raw, second
 
-        def regroup(raw, second, g, first_row, target, on_vector):
-            bank = bank_pool.tile([P, 2, BANK_ROWS * P], F32)
+        def regroup(raw, second, g, target, copy):
+            bank = bank_pool.tile([P, 2, BLOCK], F32)
             for u in range(2):
-                for j in range(BANK_ROWS):
-                    row = first_row + j
+                for j in range(BLOCK_ROWS):
                     if g < PLAIN_PASSES:
-                        words = raw[:, row, g * K_PASS : (g + 1) * K_PASS].bitcast(F32)[:, u::2]
+                        words = raw[:, j, g * K_PASS : (g + 1) * K_PASS].bitcast(F32)[:, u::2]
                     else:
-                        half = (raw[:, row, PLAIN_K:], second[:, row, :])[u].bitcast(F32)
+                        half = (raw[:, j, PLAIN_K:], second[:, j, :])[u].bitcast(F32)
                         words = half[:, (g - PLAIN_PASSES) * P : (g - PLAIN_PASSES + 1) * P]
                     nc.tensor.transpose(bank[:, u, j * P : (j + 1) * P], words, identity[:])
-            copy = nc.vector.tensor_copy if on_vector else nc.scalar.copy
             copy(
                 out=target.bitcast(F32).rearrange("p (r u) -> p r u", u=2),
                 in_=bank[:].rearrange("p u r -> p r u"),
@@ -213,36 +207,20 @@ def tile_internattention_pa_kernel(tc, x, w_qkv, q_norm_w, k_norm_w, out_0, out_
 
         ctx.enter_context(tc.manual_schedule())
 
-        nc.sync.dma_start(out=x_raw[:], in_=x_rows.rearrange("(p j) k -> p j k", j=TOKEN_TILES))
-        raws = [load_chunk(0)]
+        x_raw = load_block(x_rows)
+        raws = [load_weights(0)]
         load_gains()
-        for c in range(1, CHUNKS_AHEAD):
-            raws.append(load_chunk(c))
+        for s in range(1, BLOCKS_AHEAD):
+            raws.append(load_weights(s))
 
-        sort_rows(x_raw[:], x_second[:])
-        passes = list(range(PASSES))
-        x_grouped = const.tile([P, PASSES, TOKENS * PACK], BF16, align_bytes=64)
-        for g in passes:
-            regroup(x_raw, x_second, g, 0, x_grouped[:, g, :], g % 2 == 1)
-        ordered = {}
-        ordered[0] = (raws[0], second_pool.tile([P, ROWS, SORTED_K // 2], BF16, name="second"))
-        for first in range(0, ROWS, BANK_ROWS):
-            here = slice(first, first + BANK_ROWS)
-            sort_rows(ordered[0][0][:, here, :], ordered[0][1][:, here, :])
-            if first == 0:
-                quantise(x_grouped[:].rearrange("p g c -> p (g c)"), x_codes, x_scales, passes)
-
-        def passes_of(s):
-            first = s % STEPS_PER_CHUNK * STEP_PASSES
-            return list(range(first, first + STEP_PASSES))
-
-        def banks_of(s):
-            if s < STEPS_PER_CHUNK:
-                return [(g, s * BANK_ROWS) for g in range(PASSES)]
-            return [(g, first) for g in passes_of(s) for first in range(0, ROWS, BANK_ROWS)]
-
-        def vector_banks(s):
-            return (1, 3) if s == STEPS - 1 else ()
+        copies = (nc.scalar.copy, nc.vector.tensor_copy)
+        x_sorted = sort_block(x_raw)
+        x_grouped = grouped_pool.tile([P, PASSES, BLOCK * PACK], BF16, align_bytes=64, name="grouped")
+        for g in range(PASSES):
+            regroup(*x_sorted, g, x_grouped[:, g, :], copies[g % 2])
+        in_order = {0: sort_block(raws[0])}
+        quantise(x_grouped[:].rearrange("p g c -> p (g c)"), x_codes, x_scales, range(PASSES))
+        in_order[1] = sort_block(raws[1])
 
         grouped = {}
         operands = {}
@@ -251,23 +229,21 @@ def tile_internattention_pa_kernel(tc, x, w_qkv, q_norm_w, k_norm_w, out_0, out_
         normed = {}
         inverse = {}
         for s in range(STEPS + TAKE_LAG):
-            c = s // STEPS_PER_CHUNK
-            if s % STEPS_PER_CHUNK == 0 and c + CHUNKS_AHEAD < CHUNKS:
-                raws.append(load_chunk(c + CHUNKS_AHEAD))
+            if s + BLOCKS_AHEAD < STEPS:
+                raws.append(load_weights(s + BLOCKS_AHEAD))
 
-            done = s - QUANTISE_LAG
-            if 0 <= done < STEPS:
-                c = done // STEPS_PER_CHUNK
-                if done % STEPS_PER_CHUNK == 0:
+            if 0 <= s - QUANTISE_LAG < STEPS:
+                c, half = divmod(s - QUANTISE_LAG, BLOCKS)
+                if half == 0:
                     codes = codes_pool.tile([P, PASSES, CHUNK], U32, align_bytes=64)
                     scales = codes_pool.tile([P, PASSES, CHUNK], U8, align_bytes=64)
                     operands[c] = (codes, scales)
-                half = grouped[c, done % STEPS_PER_CHUNK]
-                if done < STEPS - 1:
-                    quantise(half[:].rearrange("p g c -> p (g c)"), *operands[c], passes_of(done))
+                passes = range(half * PASSES_AT_ONCE, (half + 1) * PASSES_AT_ONCE)
+                if s - QUANTISE_LAG < STEPS - 1:
+                    quantise(grouped[c, half][:].rearrange("p g c -> p (g c)"), *operands[c], passes)
                 else:
-                    for i in range(STEP_PASSES):
-                        quantise(half[:, i, :], *operands[c], passes_of(done)[i : i + 1])
+                    for i in range(PASSES_AT_ONCE):
+                        quantise(grouped[c, half][:, i, :], *operands[c], passes[i : i + 1])
 
             job = s - TAKE_LAG
             if 0 <= job < STEPS:
@@ -289,21 +265,23 @@ def tile_internattention_pa_kernel(tc, x, w_qkv, q_norm_w, k_norm_w, out_0, out_
                 if part > 0 and 1 <= n <= 2:
                     divide(part - 1, n - 1, inverse[part - 1], normed[part - 1])
 
-            c = s // STEPS_PER_CHUNK
             if s < STEPS:
-                for n, (g, first) in enumerate(banks_of(s)):
-                    half = (c, g // STEP_PASSES)
-                    if half not in grouped:
-                        grouped[half] = grouped_pool.tile(
-                            [P, STEP_PASSES, CHUNK * PACK], BF16, align_bytes=64, name="grouped"
+                c, block = divmod(s, BLOCKS)
+                if block == 0:
+                    for half in range(BLOCKS):
+                        grouped[c, half] = grouped_pool.tile(
+                            [P, PASSES_AT_ONCE, CHUNK * PACK], BF16, align_bytes=64, name="grouped"
                         )
-                    target = grouped[half][:, g % STEP_PASSES, first * P * PACK : (first + BANK_ROWS) * P * PACK]
-                    regroup(*ordered[c], g, first, target, n in vector_banks(s))
+                columns = slice(block * BLOCK * PACK, (block + 1) * BLOCK * PACK)
+                for g in range(PASSES):
+                    half, i = divmod(g, PASSES_AT_ONCE)
+                    copy = copies[g % 2] if s == STEPS - 1 else nc.scalar.copy
+                    regroup(*in_order[s], g, grouped[c, half][:, i, columns], copy)
 
             if 1 <= s <= NORMED_PARTS:
                 spread_gain(s - 1)
-            if s % STEPS_PER_CHUNK == 0 and c + 1 < CHUNKS:
-                ordered[c + 1] = sort_chunk(raws[c + 1])
+            if s + SORT_LEAD < STEPS:
+                in_order[s + SORT_LEAD] = sort_block(raws[s + SORT_LEAD])
 
             job = s - MULTIPLY_LAG
             if 0 <= job < STEPS:

@@ -95,22 +95,21 @@ def tile_internattention_pa_kernel(tc, x, w_qkv, q_norm_w, k_norm_w, out_0, out_
         minus_half = const.tile([P, TOKEN_TILES, 1], F32)
         nc.gpsimd.memset(minus_half[:], -0.5)
 
-        def spread_gain(part):
-            for half in range(2):
-                bank = bank_pool.tile([P, 2, CHUNK], BF16)
-                for i in range(2):
-                    row = part * CHUNKS_PER_PART + half * 2 + i
-                    nc.tensor.matmul(
-                        out=bank[:, i, :],
-                        lhsT=selectors[:, row : row + 1].to_broadcast([P, P]),
-                        rhs=gain_rows[:],
-                        start=True,
-                        stop=True,
-                    )
-                nc.vector.tensor_copy(
-                    out=gains[part][:, half * 2 * CHUNK : (half + 1) * 2 * CHUNK],
-                    in_=bank[:].rearrange("p i n -> p (i n)"),
+        def spread_gain(part, half):
+            bank = bank_pool.tile([P, 2, CHUNK], BF16)
+            for i in range(2):
+                row = part * CHUNKS_PER_PART + half * 2 + i
+                nc.tensor.matmul(
+                    out=bank[:, i, :],
+                    lhsT=selectors[:, row : row + 1].to_broadcast([P, P]),
+                    rhs=gain_rows[:],
+                    start=True,
+                    stop=True,
                 )
+            nc.vector.tensor_copy(
+                out=gains[part][:, half * 2 * CHUNK : (half + 1) * 2 * CHUNK],
+                in_=bank[:].rearrange("p i n -> p (i n)"),
+            )
 
         def load_block(rows):
             raw = raw_pool.tile([P, BLOCK_ROWS, HIDDEN], BF16)
@@ -275,11 +274,11 @@ def tile_internattention_pa_kernel(tc, x, w_qkv, q_norm_w, k_norm_w, out_0, out_
                 columns = slice(block * BLOCK * PACK, (block + 1) * BLOCK * PACK)
                 for g in range(PASSES):
                     half, i = divmod(g, PASSES_AT_ONCE)
+                    if g == PASSES - 1 and 1 <= s <= 2 * NORMED_PARTS:
+                        spread_gain(*divmod(s - 1, 2))
                     copy = copies[g % 2] if s == STEPS - 1 else nc.scalar.copy
                     regroup(*in_order[s], g, grouped[c, half][:, i, columns], copy)
 
-            if 1 <= s <= NORMED_PARTS:
-                spread_gain(s - 1)
             if s + SORT_LEAD < STEPS:
                 in_order[s + SORT_LEAD] = sort_block(raws[s + SORT_LEAD])
 

@@ -177,11 +177,15 @@ def tile_internattention_pa_kernel(tc, x, w_qkv, q_norm_w, k_norm_w, out_0, out_
             )
 
         def take_plain(acc, t, i):
-            columns = slice(i * CHUNK, (i + 1) * CHUNK)
             plain = plain_pool.tile([P, CHUNK], F32)
-            copy = nc.vector.tensor_copy if i == CHUNKS_PER_PART - 1 and t == 1 else nc.scalar.copy
-            copy(out=as_stored(plain[:]), in_=as_multiplied(acc[:]))
-            nc.sync.dma_start(out=outs[PARTS - 1][:, t, columns], in_=plain[:])
+            if i == CHUNKS_PER_PART - 1 and t == TOKEN_TILES - 1:
+                pieces = [(slice(0, BLOCK), nc.scalar.copy), (slice(BLOCK, CHUNK), nc.vector.tensor_copy)]
+            else:
+                pieces = [(slice(0, CHUNK), nc.scalar.copy)]
+            for here, copy in pieces:
+                copy(out=as_stored(plain[:, here]), in_=as_multiplied(acc[:, here]))
+                columns = slice(i * CHUNK + here.start, i * CHUNK + here.stop)
+                nc.sync.dma_start(out=outs[PARTS - 1][:, t, columns], in_=plain[:, here])
 
         def invert_root_mean_square(sumsq):
             pairs = stats_pool.tile([P, TOKEN_TILES, 2], F32)
@@ -212,11 +216,10 @@ def tile_internattention_pa_kernel(tc, x, w_qkv, q_norm_w, k_norm_w, out_0, out_
         for s in range(1, BLOCKS_AHEAD):
             raws.append(load_weights(s))
 
-        copies = (nc.scalar.copy, nc.vector.tensor_copy)
         x_sorted = sort_block(x_raw)
         x_grouped = grouped_pool.tile([P, PASSES, BLOCK * PACK], BF16, align_bytes=64, name="grouped")
         for g in range(PASSES):
-            regroup(*x_sorted, g, x_grouped[:, g, :], copies[g % 2])
+            regroup(*x_sorted, g, x_grouped[:, g, :], nc.scalar.copy)
         in_order = {0: sort_block(raws[0])}
         quantise(x_grouped[:].rearrange("p g c -> p (g c)"), x_codes, x_scales, range(PASSES))
         in_order[1] = sort_block(raws[1])
@@ -276,7 +279,7 @@ def tile_internattention_pa_kernel(tc, x, w_qkv, q_norm_w, k_norm_w, out_0, out_
                     half, i = divmod(g, PASSES_AT_ONCE)
                     if g == PASSES - 1 and 1 <= s <= 2 * NORMED_PARTS:
                         spread_gain(*divmod(s - 1, 2))
-                    copy = copies[g % 2] if s == STEPS - 1 else nc.scalar.copy
+                    copy = nc.vector.tensor_copy if s == STEPS - 1 and g % 2 == 1 else nc.scalar.copy
                     regroup(*in_order[s], g, grouped[c, half][:, i, columns], copy)
 
             if s + SORT_LEAD < STEPS:

from contextlib import ExitStack

import concourse.mybir as mybir
from concourse.masks import make_identity

F32 = mybir.dt.float32
BF16 = mybir.dt.bfloat16
U32 = mybir.dt.uint32
U8 = mybir.dt.uint8
I32 = mybir.dt.int32
FP8X4 = mybir.dt.float8_e4m3fn_x4
ALU = mybir.AluOpType
ACT = mybir.ActivationFunctionType

P = 128
HIDDEN = 2048
TOKENS = 256
EPS = 1e-6
PACK = 4
K_PASS = P * PACK
PASSES = HIDDEN // K_PASS
PLAIN_PASSES = 1
PLAIN_K = PLAIN_PASSES * K_PASS
SORTED_K = HIDDEN - PLAIN_K
RUN = 16
TOKEN_TILES = TOKENS // P
CHUNK = 512
BLOCK = 256
BLOCK_ROWS = BLOCK // P
BLOCKS = CHUNK // BLOCK
CHUNKS_PER_PART = HIDDEN // CHUNK
PARTS = 3
NORMED_PARTS = 2
CHUNKS = PARTS * CHUNKS_PER_PART
STEPS = CHUNKS * BLOCKS
SORT_LEAD = 2
BLOCKS_AHEAD = 9
PASSES_AT_ONCE = PASSES // BLOCKS
QUANTISE_LAG = 2
MULTIPLY_LAG = 4
TAKE_LAG = 5

FLOPS = 2 * TOKENS * HIDDEN * PARTS * HIDDEN


def as_multiplied(columns):
    return columns.rearrange("m (h j p) -> m h p j", j=BLOCK_ROWS, p=P)


def as_stored(columns):
    return columns.rearrange("m (h p j) -> m h p j", j=BLOCK_ROWS, p=P)


def tile_internattention_pa_kernel(tc, x, w_qkv, q_norm_w, k_norm_w, out_0, out_1, out_2):
    nc = tc.nc
    x_rows = x.flatten_outer_dims()
    outs = [
        out.flatten_outer_dims().rearrange("(p t) n -> p t n", t=TOKEN_TILES)
        for out in (out_0, out_1, out_2)
    ]
    gain_vectors = [q_norm_w, k_norm_w]

    with ExitStack() as ctx:
        const = ctx.enter_context(tc.tile_pool(name="const", bufs=1))
        raw_pool = ctx.enter_context(tc.tile_pool(name="raw", bufs=BLOCKS_AHEAD + 1))
        second_pool = ctx.enter_context(tc.tile_pool(name="second", bufs=4))
        grouped_pool = ctx.enter_context(tc.tile_pool(name="grouped", bufs=5))
        codes_pool = ctx.enter_context(tc.tile_pool(name="codes", bufs=3))
        normed_pool = ctx.enter_context(tc.tile_pool(name="normed", bufs=NORMED_PARTS * TOKEN_TILES))
        plain_pool = ctx.enter_context(tc.tile_pool(name="plain", bufs=6))
        squares_pool = ctx.enter_context(tc.tile_pool(name="squares", bufs=2))
        stats_pool = ctx.enter_context(tc.tile_pool(name="stats", bufs=NORMED_PARTS))
        bank_pool = ctx.enter_context(tc.psum_pool(name="bank", bufs=6))
        acc_pool = ctx.enter_context(tc.psum_pool(name="acc", bufs=TOKEN_TILES))

        identity = const.tile([P, P], F32)
        make_identity(nc, identity[:])
        x_codes = const.tile([P, PASSES, TOKENS], U32, align_bytes=64)
        x_scales = const.tile([P, PASSES, TOKENS], U8, align_bytes=64)

        gain_rows = const.tile([P, CHUNK], BF16)
        nc.vector.memset(gain_rows[:].bitcast(I32), 0)
        gains = [const.tile([P, HIDDEN], BF16, name="gain%d" % part) for part in range(NORMED_PARTS)]
        selectors = const.tile([P, P], BF16)
        nc.gpsimd.tensor_copy(out=selectors[:], in_=identity[:])

        def load_gains():
            for part in range(NORMED_PARTS):
                first = part * CHUNKS_PER_PART
                nc.sync.dma_start(
                    out=gain_rows[first : first + CHUNKS_PER_PART, :],
                    in_=gain_vectors[part].rearrange("(c n) -> c n", c=CHUNKS_PER_PART),
                )

        minus_half = const.tile([P, TOKEN_TILES, 1], F32)
        nc.gpsimd.memset(minus_half[:], -0.5)

        def spread_gain(part, half):
            bank = bank_pool.tile([P, 2, CHUNK], BF16)
            for i in range(2):
                row = part * CHUNKS_PER_PART + half * 2 + i
                nc.tensor.matmul(
                    out=bank[:, i, :],
                    lhsT=selectors[:, row : row + 1].to_broadcast([P, P]),
                    rhs=gain_rows[:],
                    start=True,
                    stop=True,
                )
            nc.vector.tensor_copy(
                out=gains[part][:, half * 2 * CHUNK : (half + 1) * 2 * CHUNK],
                in_=bank[:].rearrange("p i n -> p (i n)"),
            )

        def load_block(rows):
            raw = raw_pool.tile([P, BLOCK_ROWS, HIDDEN], BF16)
            nc.sync.dma_start(out=raw[:], in_=rows.rearrange("(p j) k -> p j k", j=BLOCK_ROWS))
            return raw

        def load_weights(s):
            return load_block(w_qkv[s * BLOCK : (s + 1) * BLOCK, :])

        def sort_block(raw):
            second = second_pool.tile([P, BLOCK_ROWS, SORTED_K // 2], BF16)
            runs = raw[:, :, PLAIN_K:].rearrange("p j (h r q w) -> p j h r q w", h=2, q=2, w=RUN)
            seconds = second[:].rearrange("p j (r h w) -> p j h r w", h=2, w=RUN)
            for h in range(2):
                nc.vector.tensor_copy(out=seconds[:, :, h], in_=runs[:, :, h, :, 1])
            nc.vector.tensor_copy(out=runs[:, :, 0, :, 1], in_=runs[:, :, 1, :, 0])
            return raw, second

        def regroup(raw, second, g, target, copy):
            bank = bank_pool.tile([P, 2, BLOCK], F32)
            for u in range(2):
                for j in range(BLOCK_ROWS):
                    if g < PLAIN_PASSES:
                        words = raw[:, j, g * K_PASS : (g + 1) * K_PASS].bitcast(F32)[:, u::2]
                    else:
                        half = (raw[:, j, PLAIN_K:], second[:, j, :])[u].bitcast(F32)
                        words = half[:, (g - PLAIN_PASSES) * P : (g - PLAIN_PASSES + 1) * P]
                    nc.tensor.transpose(bank[:, u, j * P : (j + 1) * P], words, identity[:])
            copy(
                out=target.bitcast(F32).rearrange("p (r u) -> p r u", u=2),
                in_=bank[:].rearrange("p u r -> p r u"),
            )

        def quantise(grouped, codes, scales, passes):
            here = slice(passes[0], passes[-1] + 1)
            nc.vector.quantize_mx(
                out=codes[:, here, :].rearrange("p g n -> p (g n)").bitcast(FP8X4),
                scales=scales[:, here, :].rearrange("p g n -> p (g n)"),
                in_=grouped,
            )

        def multiply(t, codes, scales):
            acc = acc_pool.tile([P, CHUNK], F32)
            for g in range(PASSES):
                nc.tensor.matmul_mx(
                    out=acc[:],
                    lhsT=x_codes[:, g, t * P : (t + 1) * P].bitcast(FP8X4),
                    lhsT_scale=x_scales[:, g, t * P : (t + 1) * P],
                    rhs=codes[:, g, :].bitcast(FP8X4),
                    rhs_scale=scales[:, g, :],
                    start=(g == 0),
                    stop=(g == PASSES - 1),
                )
            return acc

        def take_normed(acc, t, part, i, sumsq, normed):
            columns = slice(i * CHUNK, (i + 1) * CHUNK)
            squares = squares_pool.tile([P, CHUNK], BF16)
            nc.scalar.activation(out=squares[:], in_=acc[:], func=ACT.Square, accum_out=sumsq[:, t, i : i + 1])
            nc.vector.tensor_tensor(
                out=as_stored(normed[t][:, columns]),
                in0=as_multiplied(acc[:]),
                in1=as_stored(gains[part][:, columns]),
                op=ALU.mult,
            )

        def take_plain(acc, t, i):
            plain = plain_pool.tile([P, CHUNK], F32)
            if i == CHUNKS_PER_PART - 1 and t == TOKEN_TILES - 1:
                pieces = [(slice(0, BLOCK), nc.scalar.copy), (slice(BLOCK, CHUNK), nc.vector.tensor_copy)]
            else:
                pieces = [(slice(0, CHUNK), nc.scalar.copy)]
            for here, copy in pieces:
                copy(out=as_stored(plain[:, here]), in_=as_multiplied(acc[:, here]))
                columns = slice(i * CHUNK + here.start, i * CHUNK + here.stop)
                nc.sync.dma_start(out=outs[PARTS - 1][:, t, columns], in_=plain[:, here])

        def invert_root_mean_square(sumsq):
            pairs = stats_pool.tile([P, TOKEN_TILES, 2], F32)
            nc.gpsimd.tensor_tensor(out=pairs[:], in0=sumsq[:, :, 0:2], in1=sumsq[:, :, 2:4], op=ALU.add)
            total = stats_pool.tile([P, TOKEN_TILES, 1], F32)
            nc.gpsimd.tensor_tensor(out=total[:], in0=pairs[:, :, 0:1], in1=pairs[:, :, 1:2], op=ALU.add)
            mean = stats_pool.tile([P, TOKEN_TILES, 1], F32)
            nc.gpsimd.tensor_scalar(
                out=mean[:], in0=total[:], scalar1=1.0 / HIDDEN, scalar2=EPS, op0=ALU.mult, op1=ALU.add
            )
            inverse = stats_pool.tile([P, TOKEN_TILES, 1], F32)
            nc.gpsimd.tensor_tensor(out=inverse[:], in0=mean[:], in1=minus_half[:], op=ALU.pow)
            return inverse

        def divide(part, half, inverse, normed):
            columns = slice(half * HIDDEN // 2, (half + 1) * HIDDEN // 2)
            for t in range(TOKEN_TILES):
                nc.vector.tensor_scalar_mul(
                    out=normed[t][:, columns], in0=normed[t][:, columns], scalar1=inverse[:, t, :]
                )
                nc.sync.dma_start(out=outs[part][:, t, columns], in_=normed[t][:, columns])

        ctx.enter_context(tc.manual_schedule())

        x_raw = load_block(x_rows)
        raws = [load_weights(0)]
        load_gains()
        for s in range(1, BLOCKS_AHEAD):
            raws.append(load_weights(s))

        x_sorted = sort_block(x_raw)
        x_grouped = grouped_pool.tile([P, PASSES, BLOCK * PACK], BF16, align_bytes=64, name="grouped")
        for g in range(PASSES):
            regroup(*x_sorted, g, x_grouped[:, g, :], nc.scalar.copy)
        in_order = {0: sort_block(raws[0])}
        quantise(x_grouped[:].rearrange("p g c -> p (g c)"), x_codes, x_scales, range(PASSES))
        in_order[1] = sort_block(raws[1])

        grouped = {}
        operands = {}
        accs = {}
        sumsq = {}
        normed = {}
        inverse = {}
        for s in range(STEPS + TAKE_LAG):
            if s + BLOCKS_AHEAD < STEPS:
                raws.append(load_weights(s + BLOCKS_AHEAD))

            if 0 <= s - QUANTISE_LAG < STEPS:
                c, half = divmod(s - QUANTISE_LAG, BLOCKS)
                if half == 0:
                    codes = codes_pool.tile([P, PASSES, CHUNK], U32, align_bytes=64)
                    scales = codes_pool.tile([P, PASSES, CHUNK], U8, align_bytes=64)
                    operands[c] = (codes, scales)
                passes = range(half * PASSES_AT_ONCE, (half + 1) * PASSES_AT_ONCE)
                if s - QUANTISE_LAG < STEPS - 1:
                    quantise(grouped[c, half][:].rearrange("p g c -> p (g c)"), *operands[c], passes)
                else:
                    for i in range(PASSES_AT_ONCE):
                        quantise(grouped[c, half][:, i, :], *operands[c], passes[i : i + 1])

            job = s - TAKE_LAG
            if 0 <= job < STEPS:
                t = job % TOKEN_TILES
                part = job // TOKEN_TILES // CHUNKS_PER_PART
                i = job // TOKEN_TILES % CHUNKS_PER_PART
                if part < NORMED_PARTS:
                    if i == 0 and t == 0:
                        sumsq[part] = stats_pool.tile([P, TOKEN_TILES, CHUNKS_PER_PART], F32, name="sumsq")
                        normed[part] = [
                            normed_pool.tile([P, HIDDEN], F32, name="normed") for each in range(TOKEN_TILES)
                        ]
                    take_normed(accs[job], t, part, i, sumsq[part], normed[part])
                    if job % (TOKEN_TILES * CHUNKS_PER_PART) == TOKEN_TILES * CHUNKS_PER_PART - 1:
                        inverse[part] = invert_root_mean_square(sumsq[part])
                else:
                    take_plain(accs[job], t, i)
                n = job % (TOKEN_TILES * CHUNKS_PER_PART)
                if part > 0 and 1 <= n <= 2:
                    divide(part - 1, n - 1, inverse[part - 1], normed[part - 1])

            if s < STEPS:
                c, block = divmod(s, BLOCKS)
                if block == 0:
                    for half in range(BLOCKS):
                        grouped[c, half] = grouped_pool.tile(
                            [P, PASSES_AT_ONCE, CHUNK * PACK], BF16, align_bytes=64, name="grouped"
                        )
                columns = slice(block * BLOCK * PACK, (block + 1) * BLOCK * PACK)
                for g in range(PASSES):
                    half, i = divmod(g, PASSES_AT_ONCE)
                    if g == PASSES - 1 and 1 <= s <= 2 * NORMED_PARTS:
                        spread_gain(*divmod(s - 1, 2))
                    copy = nc.vector.tensor_copy if s == STEPS - 1 and g % 2 == 1 else nc.scalar.copy
                    regroup(*in_order[s], g, grouped[c, half][:, i, columns], copy)

            if s + SORT_LEAD < STEPS:
                in_order[s + SORT_LEAD] = sort_block(raws[s + SORT_LEAD])

            job = s - MULTIPLY_LAG
            if 0 <= job < STEPS:
                accs[job] = multiply(job % TOKEN_TILES, *operands[job // TOKEN_TILES])
